import numpy as np
import ml_dtypes


def mxq(x, axis, fmt="e4m3"):
    dtype, down = {"e4m3": (ml_dtypes.float8_e4m3fn, 7), "e5m2": (ml_dtypes.float8_e5m2, 14)}[fmt]
    v = np.moveaxis(np.asarray(x, np.float32).astype(ml_dtypes.bfloat16).astype(np.float64), axis, -1)
    blocks = v.reshape(v.shape[:-1] + (-1, 32))
    amax = np.abs(blocks).max(-1, keepdims=True)
    byte = np.maximum(np.where(amax > 0, np.frexp(amax)[1] - 1 + 127, 0) - down, 1)
    scale = np.exp2(byte - 127.0)
    codes = (blocks / scale).astype(np.float32).astype(dtype).astype(np.float64)
    return np.moveaxis((codes * scale).reshape(v.shape), -1, axis)


WIDE = False


def mx_kscale(k):
    if not WIDE:
        return np.ones(k)
    levels = np.array([10, -10, 5, -5, 0])
    if k % 512:
        return np.exp2(np.random.permutation(np.resize(levels, k // 32))).repeat(32)
    a = np.empty((k // 512, 16))
    for p in range(k // 512):
        a[p, :8] = np.random.permutation(np.resize(levels, 8))
        for g in range(8):
            far = levels[np.abs(levels - a[p, g]) >= 10]
            a[p, g + 8] = far[np.random.randint(len(far))]
    return np.exp2(a.ravel()).repeat(32)


BF16 = ml_dtypes.bfloat16


def bf(x):
    return np.asarray(x, np.float32).astype(BF16)


def f64(x):
    return np.asarray(x).astype(np.float64)


B, SIDE, HE, Z, HD, XO = 128, 32, 512, 8192, 1024, 1024


def setup_inputs():
    n = np.random.standard_normal
    s, t = mx_kscale(HE), mx_kscale(Z)
    return {"h": bf(np.tanh(n((B, HE))) * s),
            "W_mu_e": bf(n((Z, HE)) * 1.5 / np.sqrt(HE) / s[None, :] * t[:, None]),
            "b_mu_e": bf(n(Z) * 0.3 * t),
            "W_ls_e": bf(n((Z, HE)) * 1.5 / np.sqrt(HE) / s[None, :]),
            "b_ls_e": bf(n(Z) * 0.3),
            "eps_z": bf(n((B, Z)) * t),
            "W_in_d": bf(n((HD, Z)) * 0.6 / np.sqrt(Z) / t[None, :]),
            "b_in_d": bf(n(HD) * 0.3)}


def reference(h, W_mu_e, b_mu_e, W_ls_e, b_ls_e, eps_z, W_in_d, b_in_d):
    hq = mxq(f64(h), 1, "e4m3")
    mu_e = (hq @ mxq(f64(W_mu_e), 1, "e4m3").T) + f64(b_mu_e)
    ls_e = (hq @ mxq(f64(W_ls_e), 1, "e4m3").T) + f64(b_ls_e)
    z = mu_e + np.exp(0.5 * ls_e) * f64(eps_z)
    return np.tanh((mxq(z, 1, "e4m3") @ mxq(f64(W_in_d), 1, "e4m3").T) + f64(b_in_d))

@@ -1,0 +1,284 @@
+from contextlib import ExitStack
+
+import concourse.mybir as mybir
+from concourse.masks import make_identity
+
+F32 = mybir.dt.float32
+BF16 = mybir.dt.bfloat16
+U32 = mybir.dt.uint32
+U8 = mybir.dt.uint8
+FP8X4 = mybir.dt.float8_e4m3fn_x4
+ACT = mybir.ActivationFunctionType
+ALU = mybir.AluOpType
+
+P = 128
+PACK = 4
+K_PASS = P * PACK
+HIDDEN = 512
+LATENT = 8192
+OUT = 1024
+Z_PASSES = LATENT // K_PASS
+N_BLOCKS = OUT // P
+UNIT_WORDS = 8 * P
+STEPS = Z_PASSES + 2 * N_BLOCKS
+W_BUFS = 6
+D_BUFS = 5
+
+FLOPS = 2 * P * (2 * HIDDEN * LATENT + LATENT * OUT)
+
+
+def tile_vae_pa_k_kernel(tc, h, W_mu_e, b_mu_e, W_ls_e, b_ls_e, eps_z, W_in_d, b_in_d, out):
+    nc = tc.nc
+    with ExitStack() as ctx:
+        ctx.enter_context(tc.manual_schedule())
+        keep = ctx.enter_context(tc.tile_pool(name="keep", bufs=1))
+        w_pool = ctx.enter_context(tc.tile_pool(name="w_pool", bufs=W_BUFS))
+        d_pool = ctx.enter_context(tc.tile_pool(name="d_pool", bufs=D_BUFS))
+        grouped_pool = ctx.enter_context(tc.tile_pool(name="grouped_pool", bufs=4))
+        packed_pool = ctx.enter_context(tc.tile_pool(name="packed_pool", bufs=4))
+        sample_pool = ctx.enter_context(tc.tile_pool(name="sample_pool", bufs=2))
+        xt_pool = ctx.enter_context(tc.psum_pool(name="xt_pool", bufs=4))
+        acc_pool = ctx.enter_context(tc.psum_pool(name="acc_pool", bufs=2))
+        ls_pool = ctx.enter_context(tc.psum_pool(name="ls_pool", bufs=1))
+        eps_pool = ctx.enter_context(tc.psum_pool(name="eps_pool", bufs=1))
+
+        ident = keep.tile([P, P], F32)
+        make_identity(nc, ident[:])
+        ones = keep.tile([P, P], BF16)
+        nc.vector.memset(ones[:], 1.0)
+        bias_rows = keep.tile([P, K_PASS], BF16)
+        nc.vector.memset(bias_rows[:], 0.0)
+        b_in_row = keep.tile([P, OUT], BF16)
+        nc.vector.memset(b_in_row[:], 0.0)
+
+        h_raw = keep.tile([P, HIDDEN], BF16)
+        nc.sync.dma_start(out=h_raw[:], in_=h[:, :])
+        eps_raw = keep.tile([P, LATENT], BF16)
+        mu_rows = W_mu_e.rearrange("(g p t) k -> p g t k", p=P, t=PACK)
+        ls_rows = W_ls_e.rearrange("(g p t) k -> p g t k", p=P, t=PACK)
+        w_raw = {}
+        for g in range(Z_PASSES):
+            w_raw[g] = w_pool.tile([P, 2, PACK, HIDDEN], BF16, name="w_raw")
+            nc.sync.dma_start(out=w_raw[g][:, 0, :, :], in_=mu_rows[:, g, :, :])
+            nc.sync.dma_start(out=w_raw[g][:, 1, :, :], in_=ls_rows[:, g, :, :])
+            if g == 0:
+                nc.sync.dma_start(out=bias_rows[0:Z_PASSES, :], in_=b_mu_e.rearrange("(g x) -> g x", x=K_PASS))
+                nc.sync.dma_start(out=bias_rows[Z_PASSES : 2 * Z_PASSES, :], in_=b_ls_e.rearrange("(g x) -> g x", x=K_PASS))
+                nc.sync.dma_start(out=b_in_row[0:1, :], in_=b_in_d.rearrange("(o n) -> o n", o=1))
+            if g % 4 == 0:
+                quarter = slice(g * K_PASS, (g + 4) * K_PASS)
+                nc.sync.dma_start(out=eps_raw[:, quarter], in_=eps_z[:, quarter])
+        d_raw = {}
+        for nb in range(N_BLOCKS):
+            d_raw[nb] = d_pool.tile([P, LATENT], BF16, name="d_raw")
+            for half in range(2):
+                cols = slice(half * LATENT // 2, (half + 1) * LATENT // 2)
+                nc.sync.dma_start(out=d_raw[nb][:, cols], in_=W_in_d[nb * P : (nb + 1) * P, cols])
+
+        def transpose_unit(words, last_copy_on_vector):
+            grouped = grouped_pool.tile([P, PACK * K_PASS], BF16, align_bytes=64)
+            grouped_words = grouped[:].bitcast(F32).rearrange("q (j c half) -> q j c half", j=4, half=2)
+            for bank in range(2):
+                xt = xt_pool.tile([P, 2, 2, P], F32)
+                for j in range(2):
+                    for half in range(2):
+                        first = (2 * bank + j) * 2 * P
+                        nc.tensor.transpose(xt[:, j, half, :], words[:, first + half : first + 2 * P : 2], ident[:])
+                copy_out = nc.vector.tensor_copy if (last_copy_on_vector and bank == 1) else nc.scalar.copy
+                copy_out(
+                    out=grouped_words[:, 2 * bank : 2 * bank + 2, :, :],
+                    in_=xt[:].rearrange("q j half c -> q j c half"),
+                )
+            return grouped
+
+        def quantise_unit(grouped):
+            codes = packed_pool.tile([P, K_PASS], U32, align_bytes=64)
+            scales = packed_pool.tile([P, K_PASS], U8, align_bytes=64)
+            nc.vector.quantize_mx(out=codes[:].bitcast(FP8X4), scales=scales[:], in_=grouped[:])
+            return codes, scales
+
+        def step_units(step):
+            if step < Z_PASSES:
+                return [w_raw[step][:, w, :, :].rearrange("p t k -> p (t k)").bitcast(F32) for w in range(2)]
+            nb, half = divmod(step - Z_PASSES, 2)
+            d_words = d_raw[nb][:].bitcast(F32)
+            return [d_words[:, (2 * half + r) * UNIT_WORDS : (2 * half + r + 1) * UNIT_WORDS] for r in range(2)]
+
+        grouped_of = {}
+        packed_of = {}
+
+        def transposes(step):
+            units = step_units(step)
+            grouped_of[step] = [
+                transpose_unit(units[0], False),
+                transpose_unit(units[1], step >= Z_PASSES),
+            ]
+
+        h_words = h_raw[:].bitcast(F32)
+        h_xt = xt_pool.tile([P, 2, 2, P], F32, tag="xt")
+        for half in range(2):
+            nc.tensor.transpose(h_xt[:, 0, half, :], h_words[:, half : 2 * P : 2], ident[:])
+        h_grouped = keep.tile([P, K_PASS], BF16, align_bytes=64)
+        nc.vector.tensor_copy(
+            out=h_grouped[:].bitcast(F32).rearrange("q (c half) -> q c half", half=2),
+            in_=h_xt[:, 0, :, :].rearrange("q half c -> q c half"),
+        )
+        transposes(0)
+        h_codes = keep.tile([P, P], U32, align_bytes=64)
+        h_scales = keep.tile([P, P], U8, align_bytes=64)
+        nc.vector.quantize_mx(out=h_codes[:].bitcast(FP8X4), scales=h_scales[:], in_=h_grouped[:])
+
+        bias_xt = xt_pool.tile([P, 2, 2, P], F32, tag="xt")
+        bias_words = bias_rows[:].bitcast(F32)
+        for half in range(2):
+            nc.tensor.transpose(bias_xt[:, 0, half, :], bias_words[:, half : 2 * P : 2], ident[:])
+        bias_pairs = bias_xt[:, 0, :, :].bitcast(BF16).rearrange("p half (r e) -> p r half e", e=2)
+        b_mu_cols = keep.tile([P, PACK * Z_PASSES], F32)
+        nc.vector.tensor_copy(out=b_mu_cols[:].rearrange("p (g half e) -> p g half e", half=2, e=2), in_=bias_pairs[:, 0:Z_PASSES, :, :])
+        half_b_ls_cols = keep.tile([P, PACK * Z_PASSES], F32)
+        nc.vector.tensor_scalar_mul(
+            out=half_b_ls_cols[:].rearrange("p (g half e) -> p g half e", half=2, e=2),
+            in0=bias_pairs[:, Z_PASSES : 2 * Z_PASSES, :, :],
+            scalar1=0.5,
+        )
+
+        b_in_all = keep.tile([P, OUT], F32)
+        for half in range(2):
+            cols = slice(half * K_PASS, (half + 1) * K_PASS)
+            b_in_ps = xt_pool.tile([P, 2, 2, P], F32, tag="xt")
+            b_in_flat = b_in_ps[:].rearrange("q j half c -> q (j half c)")
+            nc.tensor.matmul(out=b_in_flat, lhsT=ones[:], rhs=b_in_row[:, cols], start=True, stop=True)
+            nc.vector.tensor_copy(out=b_in_all[:, cols], in_=b_in_flat)
+
+        packed_of[0] = [quantise_unit(grouped_of[0][0]), quantise_unit(grouped_of[0][1])]
+
+        eps_words = eps_raw[:].bitcast(F32)
+        z_codes = keep.tile([P, Z_PASSES, P], U32, align_bytes=64)
+        z_scales = keep.tile([P, Z_PASSES, P], U8, align_bytes=64)
+        pre_tanh = keep.tile([P, OUT], F32)
+        result = keep.tile([P, OUT], F32)
+        mu_of = {}
+        ls_of = {}
+        eps_of = {}
+        std_of = {}
+        noise_of = {}
+        planes_of = {}
+        z_grouped_of = {}
+        out_ps = {}
+
+        def encode(g):
+            eps_of[g] = eps_pool.tile([P, 2, P], F32, name="eps_ps")
+            for half in range(2):
+                first = 2 * g * P
+                nc.tensor.transpose(eps_of[g][:, half, :], eps_words[:, first + half : first + 2 * P : 2], ident[:])
+            mu_of[g] = acc_pool.tile([P, PACK, P], F32, name="mu_ps", tag="acc")
+            ls_of[g] = ls_pool.tile([P, PACK, P], F32, name="ls_ps")
+            for (codes, scales), ps in zip(packed_of[g], (mu_of[g], ls_of[g])):
+                for t in range(PACK):
+                    cols = slice(t * P, (t + 1) * P)
+                    nc.tensor.matmul_mx(
+                        out=ps[:, t, :],
+                        lhsT=codes[:, cols].bitcast(FP8X4),
+                        lhsT_scale=scales[:, cols],
+                        rhs=h_codes[:].bitcast(FP8X4),
+                        rhs_scale=h_scales[:],
+                        start=True,
+                        stop=True,
+                    )
+
+        def std_dev(g):
+            std_of[g] = sample_pool.tile([P, PACK, P], F32, name="std")
+            for t in range(PACK):
+                nc.scalar.activation(
+                    out=std_of[g][:, t, :],
+                    in_=ls_of[g][:, t, :],
+                    func=ACT.Exp,
+                    bias=half_b_ls_cols[:, PACK * g + t : PACK * g + t + 1],
+                    scale=0.5,
+                )
+
+        def scale_noise(g):
+            noise_of[g] = sample_pool.tile([P, PACK, P], F32, name="noise")
+            nc.vector.tensor_tensor(
+                out=noise_of[g][:].rearrange("p (half e) b -> p half e b", e=2),
+                in0=std_of[g][:].rearrange("p (half e) b -> p half e b", e=2),
+                in1=eps_of[g][:].bitcast(BF16).rearrange("p half (b e) -> p half e b", e=2),
+                op=ALU.mult,
+            )
+
+        def add_mean(g):
+            planes_of[g] = sample_pool.tile([P, PACK, P], BF16, name="z_planes")
+            for t in range(PACK):
+                nc.vector.scalar_tensor_tensor(
+                    out=planes_of[g][:, t, :],
+                    in0=mu_of[g][:, t, :],
+                    scalar=b_mu_cols[:, PACK * g + t : PACK * g + t + 1],
+                    in1=noise_of[g][:, t, :],
+                    op0=ALU.add,
+                    op1=ALU.add,
+                )
+
+        def regroup_z(g):
+            z_grouped_of[g] = sample_pool.tile([P, P, PACK], BF16, name="z_grouped", align_bytes=64)
+            nc.vector.tensor_copy(out=z_grouped_of[g][:], in_=planes_of[g][:].rearrange("p t b -> p b t"))
+
+        def quantise_z(g):
+            nc.vector.quantize_mx(
+                out=z_codes[:, g, :].bitcast(FP8X4),
+                scales=z_scales[:, g, :],
+                in_=z_grouped_of[g][:].rearrange("p b t -> p (b t)"),
+            )
+
+        def decode(nb, half):
+            if nb not in out_ps:
+                if nb < 2:
+                    out_ps[nb] = acc_pool.tile([P, N_BLOCKS // 2, P], F32, name="out_ps", tag="acc")
+                else:
+                    out_ps[nb] = out_ps[nb - 2]
+            for r in range(2):
+                codes, scales = packed_of[Z_PASSES + 2 * nb + half][r]
+                for j in range(PACK):
+                    g = (2 * half + r) * PACK + j
+                    cols = slice(j * P, (j + 1) * P)
+                    nc.tensor.matmul_mx(
+                        out=out_ps[nb][:, nb // 2, :],
+                        lhsT=z_codes[:, g, :].bitcast(FP8X4),
+                        lhsT_scale=z_scales[:, g, :],
+                        rhs=codes[:, cols].bitcast(FP8X4),
+                        rhs_scale=scales[:, cols],
+                        start=(g == 0),
+                        stop=(g == Z_PASSES - 1),
+                    )
+
+        def finish(nb):
+            cols = slice(nb * P, (nb + 1) * P)
+            nc.vector.tensor_tensor(
+                out=pre_tanh[:, cols], in0=out_ps[nb][:, nb // 2, :], in1=b_in_all[:, cols], op=ALU.add
+            )
+            nc.scalar.activation(out=result[:, cols], in_=pre_tanh[:, cols], func=ACT.Tanh)
+            nc.sync.dma_start(out=out[:, cols], in_=result[:, cols])
+
+        for i in range(STEPS):
+            sampling = 1 <= i <= Z_PASSES
+            if i + 1 < STEPS:
+                transposes(i + 1)
+            if sampling:
+                scale_noise(i - 1)
+            if 2 <= i <= Z_PASSES + 1:
+                quantise_z(i - 2)
+            if i < Z_PASSES:
+                encode(i)
+            else:
+                decode((i - Z_PASSES) // 2, (i - Z_PASSES) % 2)
+            if sampling:
+                add_mean(i - 1)
+            if i + 1 < STEPS:
+                first_unit = quantise_unit(grouped_of[i + 1][0])
+            if sampling:
+                regroup_z(i - 1)
+            if i + 1 < STEPS:
+                packed_of[i + 1] = [first_unit, quantise_unit(grouped_of[i + 1][1])]
+            if i < Z_PASSES:
+                std_dev(i)
+            elif (i - Z_PASSES) % 2 == 1:
+                finish((i - Z_PASSES) // 2)

@@ -36,6 +36,7 @@ def tile_vae_pa_k_kernel(tc, h, W_mu_e, b_mu_e, W_ls_e, b_ls_e, eps_z, W_in_d, b
         d_pool = ctx.enter_context(tc.tile_pool(name="d_pool", bufs=D_BUFS))
         grouped_pool = ctx.enter_context(tc.tile_pool(name="grouped_pool", bufs=4))
         packed_pool = ctx.enter_context(tc.tile_pool(name="packed_pool", bufs=4))
+        sorted_pool = ctx.enter_context(tc.tile_pool(name="sorted_pool", bufs=3))
         sample_pool = ctx.enter_context(tc.tile_pool(name="sample_pool", bufs=2))
         xt_pool = ctx.enter_context(tc.psum_pool(name="xt_pool", bufs=4))
         acc_pool = ctx.enter_context(tc.psum_pool(name="acc_pool", bufs=2))
@@ -75,7 +76,7 @@ def tile_vae_pa_k_kernel(tc, h, W_mu_e, b_mu_e, W_ls_e, b_ls_e, eps_z, W_in_d, b
                 cols = slice(half * LATENT // 2, (half + 1) * LATENT // 2)
                 nc.sync.dma_start(out=d_raw[nb][:, cols], in_=W_in_d[nb * P : (nb + 1) * P, cols])
 
-        def transpose_unit(words, last_copy_on_vector):
+        def transpose_unit(words, is_sorted):
             grouped = grouped_pool.tile([P, PACK * K_PASS], BF16, align_bytes=64)
             grouped_words = grouped[:].bitcast(F32).rearrange("q (j c half) -> q j c half", j=4, half=2)
             for bank in range(2):
@@ -83,9 +84,12 @@ def tile_vae_pa_k_kernel(tc, h, W_mu_e, b_mu_e, W_ls_e, b_ls_e, eps_z, W_in_d, b
                 for j in range(2):
                     for half in range(2):
                         first = (2 * bank + j) * 2 * P
-                        nc.tensor.transpose(xt[:, j, half, :], words[:, first + half : first + 2 * P : 2], ident[:])
-                copy_out = nc.vector.tensor_copy if (last_copy_on_vector and bank == 1) else nc.scalar.copy
-                copy_out(
+                        if is_sorted:
+                            columns = slice(first + half * P, first + (half + 1) * P)
+                        else:
+                            columns = slice(first + half, first + 2 * P, 2)
+                        nc.tensor.transpose(xt[:, j, half, :], words[:, columns], ident[:])
+                nc.scalar.copy(
                     out=grouped_words[:, 2 * bank : 2 * bank + 2, :, :],
                     in_=xt[:].rearrange("q j half c -> q j c half"),
                 )
@@ -100,19 +104,26 @@ def tile_vae_pa_k_kernel(tc, h, W_mu_e, b_mu_e, W_ls_e, b_ls_e, eps_z, W_in_d, b
         def step_units(step):
             if step < Z_PASSES:
                 return [w_raw[step][:, w, :, :].rearrange("p t k -> p (t k)").bitcast(F32) for w in range(2)]
-            nb, half = divmod(step - Z_PASSES, 2)
-            d_words = d_raw[nb][:].bitcast(F32)
-            return [d_words[:, (2 * half + r) * UNIT_WORDS : (2 * half + r + 1) * UNIT_WORDS] for r in range(2)]
+            return [sorted_of[step][:, r * UNIT_WORDS : (r + 1) * UNIT_WORDS] for r in range(2)]
 
+        sorted_of = {}
         grouped_of = {}
         packed_of = {}
 
+        def sort_words(step):
+            nb, half = divmod(step - Z_PASSES, 2)
+            first = 2 * half * UNIT_WORDS
+            sorted_of[step] = sorted_pool.tile([P, 2 * UNIT_WORDS], F32, name="sorted_words")
+            nc.vector.tensor_copy(
+                out=sorted_of[step][:].rearrange("p (j half q) -> p j half q", half=2, q=P),
+                in_=d_raw[nb][:].bitcast(F32)[:, first : first + 2 * UNIT_WORDS].rearrange(
+                    "p (j q half) -> p j half q", half=2, q=P
+                ),
+            )
+
         def transposes(step):
             units = step_units(step)
-            grouped_of[step] = [
-                transpose_unit(units[0], False),
-                transpose_unit(units[1], step >= Z_PASSES),
-            ]
+            grouped_of[step] = [transpose_unit(unit, step >= Z_PASSES) for unit in units]
 
         h_words = h_raw[:].bitcast(F32)
         h_xt = xt_pool.tile([P, 2, 2, P], F32, tag="xt")
@@ -260,6 +271,8 @@ def tile_vae_pa_k_kernel(tc, h, W_mu_e, b_mu_e, W_ls_e, b_ls_e, eps_z, W_in_d, b
 
         for i in range(STEPS):
             sampling = 1 <= i <= Z_PASSES
+            if Z_PASSES <= i + 2 < STEPS:
+                sort_words(i + 2)
             if i + 1 < STEPS:
                 transposes(i + 1)
             if sampling:

@@ -19,8 +19,11 @@ LATENT = 8192
 OUT = 1024
 Z_PASSES = LATENT // K_PASS
 N_BLOCKS = OUT // P
-UNIT_WORDS = 8 * P
+PASS_WORDS = K_PASS // 2
 STEPS = Z_PASSES + 2 * N_BLOCKS
+BANKS = 4
+SORTED_BANKS = 3
+FIRST_SORTED = Z_PASSES + 3
 W_BUFS = 6
 D_BUFS = 5
 
@@ -34,9 +37,9 @@ def tile_vae_pa_k_kernel(tc, h, W_mu_e, b_mu_e, W_ls_e, b_ls_e, eps_z, W_in_d, b
         keep = ctx.enter_context(tc.tile_pool(name="keep", bufs=1))
         w_pool = ctx.enter_context(tc.tile_pool(name="w_pool", bufs=W_BUFS))
         d_pool = ctx.enter_context(tc.tile_pool(name="d_pool", bufs=D_BUFS))
+        sorted_pool = ctx.enter_context(tc.tile_pool(name="sorted_pool", bufs=3))
         grouped_pool = ctx.enter_context(tc.tile_pool(name="grouped_pool", bufs=4))
         packed_pool = ctx.enter_context(tc.tile_pool(name="packed_pool", bufs=4))
-        sorted_pool = ctx.enter_context(tc.tile_pool(name="sorted_pool", bufs=3))
         sample_pool = ctx.enter_context(tc.tile_pool(name="sample_pool", bufs=2))
         xt_pool = ctx.enter_context(tc.psum_pool(name="xt_pool", bufs=4))
         acc_pool = ctx.enter_context(tc.psum_pool(name="acc_pool", bufs=2))
@@ -53,21 +56,27 @@ def tile_vae_pa_k_kernel(tc, h, W_mu_e, b_mu_e, W_ls_e, b_ls_e, eps_z, W_in_d, b
         nc.vector.memset(b_in_row[:], 0.0)
 
         h_raw = keep.tile([P, HIDDEN], BF16)
-        nc.sync.dma_start(out=h_raw[:], in_=h[:, :])
         eps_raw = keep.tile([P, LATENT], BF16)
         mu_rows = W_mu_e.rearrange("(g p t) k -> p g t k", p=P, t=PACK)
         ls_rows = W_ls_e.rearrange("(g p t) k -> p g t k", p=P, t=PACK)
         w_raw = {}
         for g in range(Z_PASSES):
             w_raw[g] = w_pool.tile([P, 2, PACK, HIDDEN], BF16, name="w_raw")
-            nc.sync.dma_start(out=w_raw[g][:, 0, :, :], in_=mu_rows[:, g, :, :])
+            if g == 0:
+                for t in range(0, PACK, 2):
+                    nc.sync.dma_start(out=w_raw[g][:, 0, t : t + 2, :], in_=mu_rows[:, g, t : t + 2, :])
+                nc.sync.dma_start(out=h_raw[:], in_=h[:, :])
+            else:
+                nc.sync.dma_start(out=w_raw[g][:, 0, :, :], in_=mu_rows[:, g, :, :])
             nc.sync.dma_start(out=w_raw[g][:, 1, :, :], in_=ls_rows[:, g, :, :])
             if g == 0:
                 nc.sync.dma_start(out=bias_rows[0:Z_PASSES, :], in_=b_mu_e.rearrange("(g x) -> g x", x=K_PASS))
-                nc.sync.dma_start(out=bias_rows[Z_PASSES : 2 * Z_PASSES, :], in_=b_ls_e.rearrange("(g x) -> g x", x=K_PASS))
+                nc.sync.dma_start(
+                    out=bias_rows[Z_PASSES : 2 * Z_PASSES, :], in_=b_ls_e.rearrange("(g x) -> g x", x=K_PASS)
+                )
                 nc.sync.dma_start(out=b_in_row[0:1, :], in_=b_in_d.rearrange("(o n) -> o n", o=1))
-            if g % 4 == 0:
-                quarter = slice(g * K_PASS, (g + 4) * K_PASS)
+            if g % 4 == 1:
+                quarter = slice((g - 1) * K_PASS, (g + 3) * K_PASS)
                 nc.sync.dma_start(out=eps_raw[:, quarter], in_=eps_z[:, quarter])
         d_raw = {}
         for nb in range(N_BLOCKS):
@@ -76,98 +85,59 @@ def tile_vae_pa_k_kernel(tc, h, W_mu_e, b_mu_e, W_ls_e, b_ls_e, eps_z, W_in_d, b
                 cols = slice(half * LATENT // 2, (half + 1) * LATENT // 2)
                 nc.sync.dma_start(out=d_raw[nb][:, cols], in_=W_in_d[nb * P : (nb + 1) * P, cols])
 
-        def transpose_unit(words, is_sorted):
-            grouped = grouped_pool.tile([P, PACK * K_PASS], BF16, align_bytes=64)
-            grouped_words = grouped[:].bitcast(F32).rearrange("q (j c half) -> q j c half", j=4, half=2)
-            for bank in range(2):
-                xt = xt_pool.tile([P, 2, 2, P], F32)
-                for j in range(2):
-                    for half in range(2):
-                        first = (2 * bank + j) * 2 * P
-                        if is_sorted:
-                            columns = slice(first + half * P, first + (half + 1) * P)
-                        else:
-                            columns = slice(first + half, first + 2 * P, 2)
-                        nc.tensor.transpose(xt[:, j, half, :], words[:, columns], ident[:])
-                nc.scalar.copy(
-                    out=grouped_words[:, 2 * bank : 2 * bank + 2, :, :],
-                    in_=xt[:].rearrange("q j half c -> q j c half"),
-                )
-            return grouped
-
-        def quantise_unit(grouped):
-            codes = packed_pool.tile([P, K_PASS], U32, align_bytes=64)
-            scales = packed_pool.tile([P, K_PASS], U8, align_bytes=64)
-            nc.vector.quantize_mx(out=codes[:].bitcast(FP8X4), scales=scales[:], in_=grouped[:])
-            return codes, scales
-
-        def step_units(step):
-            if step < Z_PASSES:
-                return [w_raw[step][:, w, :, :].rearrange("p t k -> p (t k)").bitcast(F32) for w in range(2)]
-            return [sorted_of[step][:, r * UNIT_WORDS : (r + 1) * UNIT_WORDS] for r in range(2)]
-
         sorted_of = {}
+        bank_of = {}
         grouped_of = {}
         packed_of = {}
 
-        def sort_words(step):
+        def step_words(step):
+            if step < Z_PASSES:
+                return w_raw[step][:].rearrange("p w t k -> p (w t k)").bitcast(F32)
             nb, half = divmod(step - Z_PASSES, 2)
-            first = 2 * half * UNIT_WORDS
-            sorted_of[step] = sorted_pool.tile([P, 2 * UNIT_WORDS], F32, name="sorted_words")
+            return d_raw[nb][:, half * LATENT // 2 : (half + 1) * LATENT // 2].bitcast(F32)
+
+        def sort_words(step):
+            operands = 2 * SORTED_BANKS
+            sorted_of[step] = sorted_pool.tile([P, operands, 2, P], F32, name="sorted_words")
             nc.vector.tensor_copy(
-                out=sorted_of[step][:].rearrange("p (j half q) -> p j half q", half=2, q=P),
-                in_=d_raw[nb][:].bitcast(F32)[:, first : first + 2 * UNIT_WORDS].rearrange(
-                    "p (j q half) -> p j half q", half=2, q=P
-                ),
+                out=sorted_of[step][:],
+                in_=step_words(step)[:, : operands * PASS_WORDS].rearrange("p (j q half) -> p j half q", half=2, q=P),
             )
 
-        def transposes(step):
-            units = step_units(step)
-            grouped_of[step] = [transpose_unit(unit, step >= Z_PASSES) for unit in units]
+        def transpose_bank(step, bank):
+            xt = xt_pool.tile([P, 2, 2, P], F32)
+            bank_of[step, bank] = xt
+            for j in range(2):
+                operand = 2 * bank + j
+                for half in range(2):
+                    if step >= FIRST_SORTED and bank < SORTED_BANKS:
+                        words = sorted_of[step][:, operand, half, :]
+                    else:
+                        words = step_words(step)[:, operand * PASS_WORDS + half : (operand + 1) * PASS_WORDS : 2]
+                    nc.tensor.transpose(xt[:, j, half, :], words, ident[:])
 
-        h_words = h_raw[:].bitcast(F32)
-        h_xt = xt_pool.tile([P, 2, 2, P], F32, tag="xt")
-        for half in range(2):
-            nc.tensor.transpose(h_xt[:, 0, half, :], h_words[:, half : 2 * P : 2], ident[:])
-        h_grouped = keep.tile([P, K_PASS], BF16, align_bytes=64)
-        nc.vector.tensor_copy(
-            out=h_grouped[:].bitcast(F32).rearrange("q (c half) -> q c half", half=2),
-            in_=h_xt[:, 0, :, :].rearrange("q half c -> q c half"),
-        )
-        transposes(0)
-        h_codes = keep.tile([P, P], U32, align_bytes=64)
-        h_scales = keep.tile([P, P], U8, align_bytes=64)
-        nc.vector.quantize_mx(out=h_codes[:].bitcast(FP8X4), scales=h_scales[:], in_=h_grouped[:])
+        def copy_bank(step, bank):
+            if bank % 2 == 0:
+                grouped_of[step, bank // 2] = grouped_pool.tile([P, PACK * K_PASS], BF16, name="grouped", align_bytes=64)
+            words = grouped_of[step, bank // 2][:].bitcast(F32).rearrange("q (j c half) -> q j c half", j=4, half=2)
+            nc.scalar.copy(
+                out=words[:, 2 * (bank % 2) : 2 * (bank % 2) + 2, :, :],
+                in_=bank_of[step, bank][:].rearrange("q j half c -> q j c half"),
+            )
 
-        bias_xt = xt_pool.tile([P, 2, 2, P], F32, tag="xt")
-        bias_words = bias_rows[:].bitcast(F32)
-        for half in range(2):
-            nc.tensor.transpose(bias_xt[:, 0, half, :], bias_words[:, half : 2 * P : 2], ident[:])
-        bias_pairs = bias_xt[:, 0, :, :].bitcast(BF16).rearrange("p half (r e) -> p r half e", e=2)
-        b_mu_cols = keep.tile([P, PACK * Z_PASSES], F32)
-        nc.vector.tensor_copy(out=b_mu_cols[:].rearrange("p (g half e) -> p g half e", half=2, e=2), in_=bias_pairs[:, 0:Z_PASSES, :, :])
-        half_b_ls_cols = keep.tile([P, PACK * Z_PASSES], F32)
-        nc.vector.tensor_scalar_mul(
-            out=half_b_ls_cols[:].rearrange("p (g half e) -> p g half e", half=2, e=2),
-            in0=bias_pairs[:, Z_PASSES : 2 * Z_PASSES, :, :],
-            scalar1=0.5,
-        )
-
-        b_in_all = keep.tile([P, OUT], F32)
-        for half in range(2):
-            cols = slice(half * K_PASS, (half + 1) * K_PASS)
-            b_in_ps = xt_pool.tile([P, 2, 2, P], F32, tag="xt")
-            b_in_flat = b_in_ps[:].rearrange("q j half c -> q (j half c)")
-            nc.tensor.matmul(out=b_in_flat, lhsT=ones[:], rhs=b_in_row[:, cols], start=True, stop=True)
-            nc.vector.tensor_copy(out=b_in_all[:, cols], in_=b_in_flat)
-
-        packed_of[0] = [quantise_unit(grouped_of[0][0]), quantise_unit(grouped_of[0][1])]
+        def quantise(step, unit):
+            codes = packed_pool.tile([P, K_PASS], U32, name="codes", align_bytes=64)
+            scales = packed_pool.tile([P, K_PASS], U8, name="scales", align_bytes=64)
+            nc.vector.quantize_mx(out=codes[:].bitcast(FP8X4), scales=scales[:], in_=grouped_of[step, unit][:])
+            packed_of[step, unit] = (codes, scales)
 
         eps_words = eps_raw[:].bitcast(F32)
         z_codes = keep.tile([P, Z_PASSES, P], U32, align_bytes=64)
         z_scales = keep.tile([P, Z_PASSES, P], U8, align_bytes=64)
-        pre_tanh = keep.tile([P, OUT], F32)
-        result = keep.tile([P, OUT], F32)
+        h_codes = keep.tile([P, P], U32, align_bytes=64)
+        h_scales = keep.tile([P, P], U8, align_bytes=64)
+        b_mu_cols = keep.tile([P, PACK * Z_PASSES], F32)
+        half_b_ls_cols = keep.tile([P, PACK * Z_PASSES], F32)
         mu_of = {}
         ls_of = {}
         eps_of = {}
@@ -175,16 +145,18 @@ def tile_vae_pa_k_kernel(tc, h, W_mu_e, b_mu_e, W_ls_e, b_ls_e, eps_z, W_in_d, b
         noise_of = {}
         planes_of = {}
         z_grouped_of = {}
-        out_ps = {}
 
-        def encode(g):
+        def transpose_noise(g):
             eps_of[g] = eps_pool.tile([P, 2, P], F32, name="eps_ps")
             for half in range(2):
-                first = 2 * g * P
-                nc.tensor.transpose(eps_of[g][:, half, :], eps_words[:, first + half : first + 2 * P : 2], ident[:])
+                words = eps_words[:, g * PASS_WORDS + half : (g + 1) * PASS_WORDS : 2]
+                nc.tensor.transpose(eps_of[g][:, half, :], words, ident[:])
+
+        def encode(g):
             mu_of[g] = acc_pool.tile([P, PACK, P], F32, name="mu_ps", tag="acc")
             ls_of[g] = ls_pool.tile([P, PACK, P], F32, name="ls_ps")
-            for (codes, scales), ps in zip(packed_of[g], (mu_of[g], ls_of[g])):
+            for unit, ps in ((0, mu_of[g]), (1, ls_of[g])):
+                codes, scales = packed_of[g, unit]
                 for t in range(PACK):
                     cols = slice(t * P, (t + 1) * P)
                     nc.tensor.matmul_mx(
@@ -240,16 +212,22 @@ def tile_vae_pa_k_kernel(tc, h, W_mu_e, b_mu_e, W_ls_e, b_ls_e, eps_z, W_in_d, b
                 in_=z_grouped_of[g][:].rearrange("p b t -> p (b t)"),
             )
 
-        def decode(nb, half):
+        b_in_all = keep.tile([P, OUT], F32)
+        pre_tanh = keep.tile([P, OUT], F32)
+        result = keep.tile([P, OUT], F32)
+        out_ps = {}
+
+        def decode(step):
+            nb, half = divmod(step - Z_PASSES, 2)
             if nb not in out_ps:
                 if nb < 2:
                     out_ps[nb] = acc_pool.tile([P, N_BLOCKS // 2, P], F32, name="out_ps", tag="acc")
                 else:
                     out_ps[nb] = out_ps[nb - 2]
-            for r in range(2):
-                codes, scales = packed_of[Z_PASSES + 2 * nb + half][r]
+            for unit in range(2):
+                codes, scales = packed_of[step, unit]
                 for j in range(PACK):
-                    g = (2 * half + r) * PACK + j
+                    g = (2 * half + unit) * PACK + j
                     cols = slice(j * P, (j + 1) * P)
                     nc.tensor.matmul_mx(
                         out=out_ps[nb][:, nb // 2, :],
@@ -261,37 +239,83 @@ def tile_vae_pa_k_kernel(tc, h, W_mu_e, b_mu_e, W_ls_e, b_ls_e, eps_z, W_in_d, b
                         stop=(g == Z_PASSES - 1),
                     )
 
-        def finish(nb):
+        def add_bias(nb):
             cols = slice(nb * P, (nb + 1) * P)
             nc.vector.tensor_tensor(
                 out=pre_tanh[:, cols], in0=out_ps[nb][:, nb // 2, :], in1=b_in_all[:, cols], op=ALU.add
             )
+
+        def finish(nb):
+            cols = slice(nb * P, (nb + 1) * P)
             nc.scalar.activation(out=result[:, cols], in_=pre_tanh[:, cols], func=ACT.Tanh)
             nc.sync.dma_start(out=out[:, cols], in_=result[:, cols])
 
-        for i in range(STEPS):
-            sampling = 1 <= i <= Z_PASSES
-            if Z_PASSES <= i + 2 < STEPS:
+        for bank in range(BANKS // 2):
+            transpose_bank(0, bank)
+            copy_bank(0, bank)
+        h_words = h_raw[:].bitcast(F32)
+        h_ps = eps_pool.tile([P, 2, P], F32, name="eps_ps")
+        for half in range(2):
+            nc.tensor.transpose(h_ps[:, half, :], h_words[:, half : 2 * P : 2], ident[:])
+        h_grouped = keep.tile([P, K_PASS], BF16, align_bytes=64)
+        nc.vector.tensor_copy(
+            out=h_grouped[:].bitcast(F32).rearrange("q (c half) -> q c half", half=2),
+            in_=h_ps[:].rearrange("q half c -> q c half"),
+        )
+        quantise(0, 0)
+        nc.vector.quantize_mx(out=h_codes[:].bitcast(FP8X4), scales=h_scales[:], in_=h_grouped[:])
+        for bank in range(BANKS // 2, BANKS):
+            transpose_bank(0, bank)
+            copy_bank(0, bank)
+
+        bias_ps = eps_pool.tile([P, 2, P], F32, name="eps_ps")
+        bias_words = bias_rows[:].bitcast(F32)
+        for half in range(2):
+            nc.tensor.transpose(bias_ps[:, half, :], bias_words[:, half : 2 * P : 2], ident[:])
+        bias_pairs = bias_ps[:].bitcast(BF16).rearrange("p half (r e) -> p r half e", e=2)
+        nc.vector.tensor_copy(
+            out=b_mu_cols[:].rearrange("p (g half e) -> p g half e", half=2, e=2), in_=bias_pairs[:, 0:Z_PASSES, :, :]
+        )
+        nc.vector.tensor_scalar_mul(
+            out=half_b_ls_cols[:].rearrange("p (g half e) -> p g half e", half=2, e=2),
+            in0=bias_pairs[:, Z_PASSES : 2 * Z_PASSES, :, :],
+            scalar1=0.5,
+        )
+        quantise(0, 1)
+        for half in range(2):
+            cols = slice(half * K_PASS, (half + 1) * K_PASS)
+            b_in_ps = acc_pool.tile([P, K_PASS], F32, name="b_in_ps", tag="acc")
+            nc.tensor.matmul(out=b_in_ps[:], lhsT=ones[:], rhs=b_in_row[:, cols], start=True, stop=True)
+            nc.scalar.copy(out=b_in_all[:, cols], in_=b_in_ps[:])
+
+        for i in range(STEPS + 1):
+            done = i - 1 - Z_PASSES
+            block_done = done // 2 if done > 0 and done % 2 == 1 else None
+            if FIRST_SORTED <= i + 2 < STEPS:
                 sort_words(i + 2)
-            if i + 1 < STEPS:
-                transposes(i + 1)
-            if sampling:
+            if 1 <= i <= Z_PASSES:
+                std_dev(i - 1)
+            for bank in range(BANKS):
+                if i + 1 < STEPS:
+                    transpose_bank(i + 1, bank)
+                    copy_bank(i + 1, bank)
+                if bank == 1 and i < Z_PASSES:
+                    transpose_noise(i)
+            if 0 < i < STEPS:
+                quantise(i, 1)
+            if block_done is not None:
+                add_bias(block_done)
+                finish(block_done)
+            if 1 <= i <= Z_PASSES:
                 scale_noise(i - 1)
             if 2 <= i <= Z_PASSES + 1:
                 quantise_z(i - 2)
+            if i + 1 < STEPS:
+                quantise(i + 1, 0)
+            if 1 <= i <= Z_PASSES:
+                add_mean(i - 1)
+                regroup_z(i - 1)
             if i < Z_PASSES:
                 encode(i)
-            else:
-                decode((i - Z_PASSES) // 2, (i - Z_PASSES) % 2)
-            if sampling:
-                add_mean(i - 1)
-            if i + 1 < STEPS:
-                first_unit = quantise_unit(grouped_of[i + 1][0])
-            if sampling:
-                regroup_z(i - 1)
-            if i + 1 < STEPS:
-                packed_of[i + 1] = [first_unit, quantise_unit(grouped_of[i + 1][1])]
-            if i < Z_PASSES:
-                std_dev(i)
-            elif (i - Z_PASSES) % 2 == 1:
-                finish((i - Z_PASSES) // 2)
+            elif i < STEPS:
+                decode(i)

@@ -155,7 +155,7 @@ def tile_vae_pa_k_kernel(tc, h, W_mu_e, b_mu_e, W_ls_e, b_ls_e, eps_z, W_in_d, b
         def encode(g):
             mu_of[g] = acc_pool.tile([P, PACK, P], F32, name="mu_ps", tag="acc")
             ls_of[g] = ls_pool.tile([P, PACK, P], F32, name="ls_ps")
-            for unit, ps in ((0, mu_of[g]), (1, ls_of[g])):
+            for unit, ps in ((1, ls_of[g]), (0, mu_of[g])):
                 codes, scales = packed_of[g, unit]
                 for t in range(PACK):
                     cols = slice(t * P, (t + 1) * P)
@@ -293,28 +293,31 @@ def tile_vae_pa_k_kernel(tc, h, W_mu_e, b_mu_e, W_ls_e, b_ls_e, eps_z, W_in_d, b
             block_done = done // 2 if done > 0 and done % 2 == 1 else None
             if FIRST_SORTED <= i + 2 < STEPS:
                 sort_words(i + 2)
-            if 1 <= i <= Z_PASSES:
-                std_dev(i - 1)
             for bank in range(BANKS):
                 if i + 1 < STEPS:
                     transpose_bank(i + 1, bank)
                     copy_bank(i + 1, bank)
-                if bank == 1 and i < Z_PASSES:
-                    transpose_noise(i)
+                if bank == 0 and 1 <= i <= Z_PASSES:
+                    std_dev(i - 1)
+                if bank == 1 and 1 <= i <= Z_PASSES:
+                    transpose_noise(i - 1)
             if 0 < i < STEPS:
                 quantise(i, 1)
             if block_done is not None:
                 add_bias(block_done)
                 finish(block_done)
+            if 2 <= i <= Z_PASSES + 1:
+                add_mean(i - 2)
+            if 3 <= i <= Z_PASSES + 1:
+                quantise_z(i - 3)
+            if 2 <= i <= Z_PASSES + 1:
+                regroup_z(i - 2)
+            if i == Z_PASSES + 1:
+                quantise_z(i - 2)
             if 1 <= i <= Z_PASSES:
                 scale_noise(i - 1)
-            if 2 <= i <= Z_PASSES + 1:
-                quantise_z(i - 2)
             if i + 1 < STEPS:
                 quantise(i + 1, 0)
-            if 1 <= i <= Z_PASSES:
-                add_mean(i - 1)
-                regroup_z(i - 1)
             if i < Z_PASSES:
                 encode(i)
             elif i < STEPS:

@@ -100,8 +100,10 @@ def tile_vae_pa_k_kernel(tc, h, W_mu_e, b_mu_e, W_ls_e, b_ls_e, eps_z, W_in_d, b
             operands = 2 * SORTED_BANKS
             sorted_of[step] = sorted_pool.tile([P, operands, 2, P], F32, name="sorted_words")
             nc.vector.tensor_copy(
-                out=sorted_of[step][:],
-                in_=step_words(step)[:, : operands * PASS_WORDS].rearrange("p (j q half) -> p j half q", half=2, q=P),
+                out=sorted_of[step][:].rearrange("p j half (c x) -> p j c half x", x=4),
+                in_=step_words(step)[:, : operands * PASS_WORDS].rearrange(
+                    "p (j c x half) -> p j c half x", half=2, x=4, c=P // 4
+                ),
             )
 
         def transpose_bank(step, bank):
@@ -203,7 +205,10 @@ def tile_vae_pa_k_kernel(tc, h, W_mu_e, b_mu_e, W_ls_e, b_ls_e, eps_z, W_in_d, b
 
         def regroup_z(g):
             z_grouped_of[g] = sample_pool.tile([P, P, PACK], BF16, name="z_grouped", align_bytes=64)
-            nc.vector.tensor_copy(out=z_grouped_of[g][:], in_=planes_of[g][:].rearrange("p t b -> p b t"))
+            nc.vector.tensor_copy(
+                out=z_grouped_of[g][:].rearrange("p (c x) t -> p c t x", x=4),
+                in_=planes_of[g][:].rearrange("p t (c x) -> p c t x", x=4),
+            )
 
         def quantise_z(g):
             nc.vector.quantize_mx(

@@ -22,7 +22,7 @@ N_BLOCKS = OUT // P
 PASS_WORDS = K_PASS // 2
 STEPS = Z_PASSES + 2 * N_BLOCKS
 BANKS = 4
-SORTED_BANKS = 3
+SORTED_OPERANDS = 5
 FIRST_SORTED = Z_PASSES + 3
 W_BUFS = 6
 D_BUFS = 5
@@ -48,12 +48,9 @@ def tile_vae_pa_k_kernel(tc, h, W_mu_e, b_mu_e, W_ls_e, b_ls_e, eps_z, W_in_d, b
 
         ident = keep.tile([P, P], F32)
         make_identity(nc, ident[:])
-        ones = keep.tile([P, P], BF16)
-        nc.vector.memset(ones[:], 1.0)
         bias_rows = keep.tile([P, K_PASS], BF16)
         nc.vector.memset(bias_rows[:], 0.0)
-        b_in_row = keep.tile([P, OUT], BF16)
-        nc.vector.memset(b_in_row[:], 0.0)
+        b_in_all = keep.tile([P, OUT], BF16)
 
         h_raw = keep.tile([P, HIDDEN], BF16)
         eps_raw = keep.tile([P, LATENT], BF16)
@@ -63,8 +60,8 @@ def tile_vae_pa_k_kernel(tc, h, W_mu_e, b_mu_e, W_ls_e, b_ls_e, eps_z, W_in_d, b
         for g in range(Z_PASSES):
             w_raw[g] = w_pool.tile([P, 2, PACK, HIDDEN], BF16, name="w_raw")
             if g == 0:
-                for t in range(0, PACK, 2):
-                    nc.sync.dma_start(out=w_raw[g][:, 0, t : t + 2, :], in_=mu_rows[:, g, t : t + 2, :])
+                for t in range(PACK):
+                    nc.sync.dma_start(out=w_raw[g][:, 0, t, :], in_=mu_rows[:, g, t, :])
                 nc.sync.dma_start(out=h_raw[:], in_=h[:, :])
             else:
                 nc.sync.dma_start(out=w_raw[g][:, 0, :, :], in_=mu_rows[:, g, :, :])
@@ -74,7 +71,8 @@ def tile_vae_pa_k_kernel(tc, h, W_mu_e, b_mu_e, W_ls_e, b_ls_e, eps_z, W_in_d, b
                 nc.sync.dma_start(
                     out=bias_rows[Z_PASSES : 2 * Z_PASSES, :], in_=b_ls_e.rearrange("(g x) -> g x", x=K_PASS)
                 )
-                nc.sync.dma_start(out=b_in_row[0:1, :], in_=b_in_d.rearrange("(o n) -> o n", o=1))
+            if g == Z_PASSES // 2:
+                nc.sync.dma_start(out=b_in_all[:], in_=b_in_d.partition_broadcast(P))
             if g % 4 == 1:
                 quarter = slice((g - 1) * K_PASS, (g + 3) * K_PASS)
                 nc.sync.dma_start(out=eps_raw[:, quarter], in_=eps_z[:, quarter])
@@ -97,14 +95,13 @@ def tile_vae_pa_k_kernel(tc, h, W_mu_e, b_mu_e, W_ls_e, b_ls_e, eps_z, W_in_d, b
             return d_raw[nb][:, half * LATENT // 2 : (half + 1) * LATENT // 2].bitcast(F32)
 
         def sort_words(step):
-            operands = 2 * SORTED_BANKS
-            sorted_of[step] = sorted_pool.tile([P, operands, 2, P], F32, name="sorted_words")
-            nc.vector.tensor_copy(
-                out=sorted_of[step][:].rearrange("p j half (c x) -> p j c half x", x=4),
-                in_=step_words(step)[:, : operands * PASS_WORDS].rearrange(
-                    "p (j c x half) -> p j c half x", half=2, x=4, c=P // 4
-                ),
+            sorted_of[step] = sorted_pool.tile([P, SORTED_OPERANDS, 2, P], F32, name="sorted_words")
+            words = step_words(step)[:, : SORTED_OPERANDS * PASS_WORDS].rearrange(
+                "p (j c x half) -> p j c half x", half=2, x=4, c=P // 4
             )
+            in_order = sorted_of[step][:].rearrange("p j half (c x) -> p j c half x", x=4)
+            for some in (slice(0, PACK), slice(PACK, SORTED_OPERANDS)):
+                nc.vector.tensor_copy(out=in_order[:, some, :, :, :], in_=words[:, some, :, :, :])
 
         def transpose_bank(step, bank):
             xt = xt_pool.tile([P, 2, 2, P], F32)
@@ -112,7 +109,7 @@ def tile_vae_pa_k_kernel(tc, h, W_mu_e, b_mu_e, W_ls_e, b_ls_e, eps_z, W_in_d, b
             for j in range(2):
                 operand = 2 * bank + j
                 for half in range(2):
-                    if step >= FIRST_SORTED and bank < SORTED_BANKS:
+                    if step >= FIRST_SORTED and operand < SORTED_OPERANDS:
                         words = sorted_of[step][:, operand, half, :]
                     else:
                         words = step_words(step)[:, operand * PASS_WORDS + half : (operand + 1) * PASS_WORDS : 2]
@@ -122,7 +119,8 @@ def tile_vae_pa_k_kernel(tc, h, W_mu_e, b_mu_e, W_ls_e, b_ls_e, eps_z, W_in_d, b
             if bank % 2 == 0:
                 grouped_of[step, bank // 2] = grouped_pool.tile([P, PACK * K_PASS], BF16, name="grouped", align_bytes=64)
             words = grouped_of[step, bank // 2][:].bitcast(F32).rearrange("q (j c half) -> q j c half", j=4, half=2)
-            nc.scalar.copy(
+            copy_out = nc.vector.tensor_copy if step == STEPS - 1 and bank == 2 else nc.scalar.copy
+            copy_out(
                 out=words[:, 2 * (bank % 2) : 2 * (bank % 2) + 2, :, :],
                 in_=bank_of[step, bank][:].rearrange("q j half c -> q j c half"),
             )
@@ -217,7 +215,6 @@ def tile_vae_pa_k_kernel(tc, h, W_mu_e, b_mu_e, W_ls_e, b_ls_e, eps_z, W_in_d, b
                 in_=z_grouped_of[g][:].rearrange("p b t -> p (b t)"),
             )
 
-        b_in_all = keep.tile([P, OUT], F32)
         pre_tanh = keep.tile([P, OUT], F32)
         result = keep.tile([P, OUT], F32)
         out_ps = {}
@@ -287,12 +284,6 @@ def tile_vae_pa_k_kernel(tc, h, W_mu_e, b_mu_e, W_ls_e, b_ls_e, eps_z, W_in_d, b
             scalar1=0.5,
         )
         quantise(0, 1)
-        for half in range(2):
-            cols = slice(half * K_PASS, (half + 1) * K_PASS)
-            b_in_ps = acc_pool.tile([P, K_PASS], F32, name="b_in_ps", tag="acc")
-            nc.tensor.matmul(out=b_in_ps[:], lhsT=ones[:], rhs=b_in_row[:, cols], start=True, stop=True)
-            nc.scalar.copy(out=b_in_all[:, cols], in_=b_in_ps[:])
-
         for i in range(STEPS + 1):
             done = i - 1 - Z_PASSES
             block_done = done // 2 if done > 0 and done % 2 == 1 else None
@@ -301,12 +292,14 @@ def tile_vae_pa_k_kernel(tc, h, W_mu_e, b_mu_e, W_ls_e, b_ls_e, eps_z, W_in_d, b
             for bank in range(BANKS):
                 if i + 1 < STEPS:
                     transpose_bank(i + 1, bank)
+                    if i + 2 == STEPS and bank == 2:
+                        quantise(i, 1)
                     copy_bank(i + 1, bank)
                 if bank == 0 and 1 <= i <= Z_PASSES:
                     std_dev(i - 1)
                 if bank == 1 and 1 <= i <= Z_PASSES:
                     transpose_noise(i - 1)
-            if 0 < i < STEPS:
+            if 0 < i < STEPS and i + 2 != STEPS:
                 quantise(i, 1)
             if block_done is not None:
                 add_bias(block_done)
@@ -315,12 +308,12 @@ def tile_vae_pa_k_kernel(tc, h, W_mu_e, b_mu_e, W_ls_e, b_ls_e, eps_z, W_in_d, b
                 add_mean(i - 2)
             if 3 <= i <= Z_PASSES + 1:
                 quantise_z(i - 3)
+            if 1 <= i <= Z_PASSES:
+                scale_noise(i - 1)
             if 2 <= i <= Z_PASSES + 1:
                 regroup_z(i - 2)
             if i == Z_PASSES + 1:
                 quantise_z(i - 2)
-            if 1 <= i <= Z_PASSES:
-                scale_noise(i - 1)
             if i + 1 < STEPS:
                 quantise(i + 1, 0)
             if i < Z_PASSES:

@@ -41,7 +41,7 @@ def tile_vae_pa_k_kernel(tc, h, W_mu_e, b_mu_e, W_ls_e, b_ls_e, eps_z, W_in_d, b
         grouped_pool = ctx.enter_context(tc.tile_pool(name="grouped_pool", bufs=4))
         packed_pool = ctx.enter_context(tc.tile_pool(name="packed_pool", bufs=4))
         sample_pool = ctx.enter_context(tc.tile_pool(name="sample_pool", bufs=2))
-        xt_pool = ctx.enter_context(tc.psum_pool(name="xt_pool", bufs=4))
+        xt_pool = ctx.enter_context(tc.psum_pool(name="xt_pool", bufs=1))
         acc_pool = ctx.enter_context(tc.psum_pool(name="acc_pool", bufs=2))
         ls_pool = ctx.enter_context(tc.psum_pool(name="ls_pool", bufs=1))
         eps_pool = ctx.enter_context(tc.psum_pool(name="eps_pool", bufs=1))
@@ -104,7 +104,16 @@ def tile_vae_pa_k_kernel(tc, h, W_mu_e, b_mu_e, W_ls_e, b_ls_e, eps_z, W_in_d, b
                 nc.vector.tensor_copy(out=in_order[:, some, :, :, :], in_=words[:, some, :, :, :])
 
         def transpose_bank(step, bank):
-            xt = xt_pool.tile([P, 2, 2, P], F32)
+            pair = 2 * step + bank // 2
+            pairs = 2 if step < Z_PASSES + 2 else 3
+            swapped = pair // pairs % 2
+            place = 2 * (pair % pairs) + (bank % 2 if swapped == 0 else 1 - bank % 2)
+            if place < 4:
+                xt = xt_pool.tile([P, 2, 2, P], F32, name="xt", tag="xt%d" % place)
+            elif place == 4:
+                xt = ls_pool.tile([P, 2, 2, P], F32, name="ls_ps")
+            else:
+                xt = eps_pool.tile([P, 2, 2, P], F32, name="eps_ps")
             bank_of[step, bank] = xt
             for j in range(2):
                 operand = 2 * bank + j

from contextlib import ExitStack

import concourse.mybir as mybir
from concourse.masks import make_identity

F32 = mybir.dt.float32
BF16 = mybir.dt.bfloat16
U32 = mybir.dt.uint32
U8 = mybir.dt.uint8
FP8X4 = mybir.dt.float8_e4m3fn_x4
ACT = mybir.ActivationFunctionType
ALU = mybir.AluOpType

P = 128
PACK = 4
K_PASS = P * PACK
HIDDEN = 512
LATENT = 8192
OUT = 1024
Z_PASSES = LATENT // K_PASS
N_BLOCKS = OUT // P
PASS_WORDS = K_PASS // 2
STEPS = Z_PASSES + 2 * N_BLOCKS
BANKS = 4
SORTED_OPERANDS = 5
FIRST_SORTED = Z_PASSES + 3
W_BUFS = 6
D_BUFS = 5

FLOPS = 2 * P * (2 * HIDDEN * LATENT + LATENT * OUT)


def tile_vae_pa_k_kernel(tc, h, W_mu_e, b_mu_e, W_ls_e, b_ls_e, eps_z, W_in_d, b_in_d, out):
    nc = tc.nc
    with ExitStack() as ctx:
        ctx.enter_context(tc.manual_schedule())
        keep = ctx.enter_context(tc.tile_pool(name="keep", bufs=1))
        w_pool = ctx.enter_context(tc.tile_pool(name="w_pool", bufs=W_BUFS))
        d_pool = ctx.enter_context(tc.tile_pool(name="d_pool", bufs=D_BUFS))
        sorted_pool = ctx.enter_context(tc.tile_pool(name="sorted_pool", bufs=3))
        grouped_pool = ctx.enter_context(tc.tile_pool(name="grouped_pool", bufs=4))
        packed_pool = ctx.enter_context(tc.tile_pool(name="packed_pool", bufs=4))
        sample_pool = ctx.enter_context(tc.tile_pool(name="sample_pool", bufs=2))
        xt_pool = ctx.enter_context(tc.psum_pool(name="xt_pool", bufs=1))
        acc_pool = ctx.enter_context(tc.psum_pool(name="acc_pool", bufs=2))
        ls_pool = ctx.enter_context(tc.psum_pool(name="ls_pool", bufs=1))
        eps_pool = ctx.enter_context(tc.psum_pool(name="eps_pool", bufs=1))

        ident = keep.tile([P, P], F32)
        make_identity(nc, ident[:])
        bias_rows = keep.tile([P, K_PASS], BF16)
        nc.vector.memset(bias_rows[:], 0.0)
        b_in_all = keep.tile([P, OUT], BF16)

        h_raw = keep.tile([P, HIDDEN], BF16)
        eps_raw = keep.tile([P, LATENT], BF16)
        mu_rows = W_mu_e.rearrange("(g p t) k -> p g t k", p=P, t=PACK)
        ls_rows = W_ls_e.rearrange("(g p t) k -> p g t k", p=P, t=PACK)
        w_raw = {}
        for g in range(Z_PASSES):
            w_raw[g] = w_pool.tile([P, 2, PACK, HIDDEN], BF16, name="w_raw")
            if g == 0:
                for t in range(PACK):
                    nc.sync.dma_start(out=w_raw[g][:, 0, t, :], in_=mu_rows[:, g, t, :])
                nc.sync.dma_start(out=h_raw[:], in_=h[:, :])
            else:
                nc.sync.dma_start(out=w_raw[g][:, 0, :, :], in_=mu_rows[:, g, :, :])
            nc.sync.dma_start(out=w_raw[g][:, 1, :, :], in_=ls_rows[:, g, :, :])
            if g == 0:
                nc.sync.dma_start(out=bias_rows[0:Z_PASSES, :], in_=b_mu_e.rearrange("(g x) -> g x", x=K_PASS))
                nc.sync.dma_start(
                    out=bias_rows[Z_PASSES : 2 * Z_PASSES, :], in_=b_ls_e.rearrange("(g x) -> g x", x=K_PASS)
                )
            if g == Z_PASSES // 2:
                nc.sync.dma_start(out=b_in_all[:], in_=b_in_d.partition_broadcast(P))
            if g % 4 == 1:
                quarter = slice((g - 1) * K_PASS, (g + 3) * K_PASS)
                nc.sync.dma_start(out=eps_raw[:, quarter], in_=eps_z[:, quarter])
        d_raw = {}
        for nb in range(N_BLOCKS):
            d_raw[nb] = d_pool.tile([P, LATENT], BF16, name="d_raw")
            for half in range(2):
                cols = slice(half * LATENT // 2, (half + 1) * LATENT // 2)
                nc.sync.dma_start(out=d_raw[nb][:, cols], in_=W_in_d[nb * P : (nb + 1) * P, cols])

        sorted_of = {}
        bank_of = {}
        grouped_of = {}
        packed_of = {}

        def step_words(step):
            if step < Z_PASSES:
                return w_raw[step][:].rearrange("p w t k -> p (w t k)").bitcast(F32)
            nb, half = divmod(step - Z_PASSES, 2)
            return d_raw[nb][:, half * LATENT // 2 : (half + 1) * LATENT // 2].bitcast(F32)

        def sort_words(step):
            sorted_of[step] = sorted_pool.tile([P, SORTED_OPERANDS, 2, P], F32, name="sorted_words")
            words = step_words(step)[:, : SORTED_OPERANDS * PASS_WORDS].rearrange(
                "p (j c x half) -> p j c half x", half=2, x=4, c=P // 4
            )
            in_order = sorted_of[step][:].rearrange("p j half (c x) -> p j c half x", x=4)
            for some in (slice(0, PACK), slice(PACK, SORTED_OPERANDS)):
                nc.vector.tensor_copy(out=in_order[:, some, :, :, :], in_=words[:, some, :, :, :])

        def transpose_bank(step, bank):
            pair = 2 * step + bank // 2
            pairs = 2 if step < Z_PASSES + 2 else 3
            swapped = pair // pairs % 2
            place = 2 * (pair % pairs) + (bank % 2 if swapped == 0 else 1 - bank % 2)
            if place < 4:
                xt = xt_pool.tile([P, 2, 2, P], F32, name="xt", tag="xt%d" % place)
            elif place == 4:
                xt = ls_pool.tile([P, 2, 2, P], F32, name="ls_ps")
            else:
                xt = eps_pool.tile([P, 2, 2, P], F32, name="eps_ps")
            bank_of[step, bank] = xt
            for j in range(2):
                operand = 2 * bank + j
                for half in range(2):
                    if step >= FIRST_SORTED and operand < SORTED_OPERANDS:
                        words = sorted_of[step][:, operand, half, :]
                    else:
                        words = step_words(step)[:, operand * PASS_WORDS + half : (operand + 1) * PASS_WORDS : 2]
                    nc.tensor.transpose(xt[:, j, half, :], words, ident[:])

        def copy_bank(step, bank):
            if bank % 2 == 0:
                grouped_of[step, bank // 2] = grouped_pool.tile([P, PACK * K_PASS], BF16, name="grouped", align_bytes=64)
            words = grouped_of[step, bank // 2][:].bitcast(F32).rearrange("q (j c half) -> q j c half", j=4, half=2)
            copy_out = nc.vector.tensor_copy if step == STEPS - 1 and bank == 2 else nc.scalar.copy
            copy_out(
                out=words[:, 2 * (bank % 2) : 2 * (bank % 2) + 2, :, :],
                in_=bank_of[step, bank][:].rearrange("q j half c -> q j c half"),
            )

        def quantise(step, unit):
            codes = packed_pool.tile([P, K_PASS], U32, name="codes", align_bytes=64)
            scales = packed_pool.tile([P, K_PASS], U8, name="scales", align_bytes=64)
            nc.vector.quantize_mx(out=codes[:].bitcast(FP8X4), scales=scales[:], in_=grouped_of[step, unit][:])
            packed_of[step, unit] = (codes, scales)

        eps_words = eps_raw[:].bitcast(F32)
        z_codes = keep.tile([P, Z_PASSES, P], U32, align_bytes=64)
        z_scales = keep.tile([P, Z_PASSES, P], U8, align_bytes=64)
        h_codes = keep.tile([P, P], U32, align_bytes=64)
        h_scales = keep.tile([P, P], U8, align_bytes=64)
        b_mu_cols = keep.tile([P, PACK * Z_PASSES], F32)
        half_b_ls_cols = keep.tile([P, PACK * Z_PASSES], F32)
        mu_of = {}
        ls_of = {}
        eps_of = {}
        std_of = {}
        noise_of = {}
        planes_of = {}
        z_grouped_of = {}

        def transpose_noise(g):
            eps_of[g] = eps_pool.tile([P, 2, P], F32, name="eps_ps")
            for half in range(2):
                words = eps_words[:, g * PASS_WORDS + half : (g + 1) * PASS_WORDS : 2]
                nc.tensor.transpose(eps_of[g][:, half, :], words, ident[:])

        def encode(g):
            mu_of[g] = acc_pool.tile([P, PACK, P], F32, name="mu_ps", tag="acc")
            ls_of[g] = ls_pool.tile([P, PACK, P], F32, name="ls_ps")
            for unit, ps in ((1, ls_of[g]), (0, mu_of[g])):
                codes, scales = packed_of[g, unit]
                for t in range(PACK):
                    cols = slice(t * P, (t + 1) * P)
                    nc.tensor.matmul_mx(
                        out=ps[:, t, :],
                        lhsT=codes[:, cols].bitcast(FP8X4),
                        lhsT_scale=scales[:, cols],
                        rhs=h_codes[:].bitcast(FP8X4),
                        rhs_scale=h_scales[:],
                        start=True,
                        stop=True,
                    )

        def std_dev(g):
            std_of[g] = sample_pool.tile([P, PACK, P], F32, name="std")
            for t in range(PACK):
                nc.scalar.activation(
                    out=std_of[g][:, t, :],
                    in_=ls_of[g][:, t, :],
                    func=ACT.Exp,
                    bias=half_b_ls_cols[:, PACK * g + t : PACK * g + t + 1],
                    scale=0.5,
                )

        def scale_noise(g):
            noise_of[g] = sample_pool.tile([P, PACK, P], F32, name="noise")
            nc.vector.tensor_tensor(
                out=noise_of[g][:].rearrange("p (half e) b -> p half e b", e=2),
                in0=std_of[g][:].rearrange("p (half e) b -> p half e b", e=2),
                in1=eps_of[g][:].bitcast(BF16).rearrange("p half (b e) -> p half e b", e=2),
                op=ALU.mult,
            )

        def add_mean(g):
            planes_of[g] = sample_pool.tile([P, PACK, P], BF16, name="z_planes")
            for t in range(PACK):
                nc.vector.scalar_tensor_tensor(
                    out=planes_of[g][:, t, :],
                    in0=mu_of[g][:, t, :],
                    scalar=b_mu_cols[:, PACK * g + t : PACK * g + t + 1],
                    in1=noise_of[g][:, t, :],
                    op0=ALU.add,
                    op1=ALU.add,
                )

        def regroup_z(g):
            z_grouped_of[g] = sample_pool.tile([P, P, PACK], BF16, name="z_grouped", align_bytes=64)
            nc.vector.tensor_copy(
                out=z_grouped_of[g][:].rearrange("p (c x) t -> p c t x", x=4),
                in_=planes_of[g][:].rearrange("p t (c x) -> p c t x", x=4),
            )

        def quantise_z(g):
            nc.vector.quantize_mx(
                out=z_codes[:, g, :].bitcast(FP8X4),
                scales=z_scales[:, g, :],
                in_=z_grouped_of[g][:].rearrange("p b t -> p (b t)"),
            )

        pre_tanh = keep.tile([P, OUT], F32)
        result = keep.tile([P, OUT], F32)
        out_ps = {}

        def decode(step):
            nb, half = divmod(step - Z_PASSES, 2)
            if nb not in out_ps:
                if nb < 2:
                    out_ps[nb] = acc_pool.tile([P, N_BLOCKS // 2, P], F32, name="out_ps", tag="acc")
                else:
                    out_ps[nb] = out_ps[nb - 2]
            for unit in range(2):
                codes, scales = packed_of[step, unit]
                for j in range(PACK):
                    g = (2 * half + unit) * PACK + j
                    cols = slice(j * P, (j + 1) * P)
                    nc.tensor.matmul_mx(
                        out=out_ps[nb][:, nb // 2, :],
                        lhsT=z_codes[:, g, :].bitcast(FP8X4),
                        lhsT_scale=z_scales[:, g, :],
                        rhs=codes[:, cols].bitcast(FP8X4),
                        rhs_scale=scales[:, cols],
                        start=(g == 0),
                        stop=(g == Z_PASSES - 1),
                    )

        def add_bias(nb):
            cols = slice(nb * P, (nb + 1) * P)
            nc.vector.tensor_tensor(
                out=pre_tanh[:, cols], in0=out_ps[nb][:, nb // 2, :], in1=b_in_all[:, cols], op=ALU.add
            )

        def finish(nb):
            cols = slice(nb * P, (nb + 1) * P)
            nc.scalar.activation(out=result[:, cols], in_=pre_tanh[:, cols], func=ACT.Tanh)
            nc.sync.dma_start(out=out[:, cols], in_=result[:, cols])

        for bank in range(BANKS // 2):
            transpose_bank(0, bank)
            copy_bank(0, bank)
        h_words = h_raw[:].bitcast(F32)
        h_ps = eps_pool.tile([P, 2, P], F32, name="eps_ps")
        for half in range(2):
            nc.tensor.transpose(h_ps[:, half, :], h_words[:, half : 2 * P : 2], ident[:])
        h_grouped = keep.tile([P, K_PASS], BF16, align_bytes=64)
        nc.vector.tensor_copy(
            out=h_grouped[:].bitcast(F32).rearrange("q (c half) -> q c half", half=2),
            in_=h_ps[:].rearrange("q half c -> q c half"),
        )
        quantise(0, 0)
        nc.vector.quantize_mx(out=h_codes[:].bitcast(FP8X4), scales=h_scales[:], in_=h_grouped[:])
        for bank in range(BANKS // 2, BANKS):
            transpose_bank(0, bank)
            copy_bank(0, bank)

        bias_ps = eps_pool.tile([P, 2, P], F32, name="eps_ps")
        bias_words = bias_rows[:].bitcast(F32)
        for half in range(2):
            nc.tensor.transpose(bias_ps[:, half, :], bias_words[:, half : 2 * P : 2], ident[:])
        bias_pairs = bias_ps[:].bitcast(BF16).rearrange("p half (r e) -> p r half e", e=2)
        nc.vector.tensor_copy(
            out=b_mu_cols[:].rearrange("p (g half e) -> p g half e", half=2, e=2), in_=bias_pairs[:, 0:Z_PASSES, :, :]
        )
        nc.vector.tensor_scalar_mul(
            out=half_b_ls_cols[:].rearrange("p (g half e) -> p g half e", half=2, e=2),
            in0=bias_pairs[:, Z_PASSES : 2 * Z_PASSES, :, :],
            scalar1=0.5,
        )
        quantise(0, 1)
        for i in range(STEPS + 1):
            done = i - 1 - Z_PASSES
            block_done = done // 2 if done > 0 and done % 2 == 1 else None
            if FIRST_SORTED <= i + 2 < STEPS:
                sort_words(i + 2)
            for bank in range(BANKS):
                if i + 1 < STEPS:
                    transpose_bank(i + 1, bank)
                    if i + 2 == STEPS and bank == 2:
                        quantise(i, 1)
                    copy_bank(i + 1, bank)
                if bank == 0 and 1 <= i <= Z_PASSES:
                    std_dev(i - 1)
                if bank == 1 and 1 <= i <= Z_PASSES:
                    transpose_noise(i - 1)
            if 0 < i < STEPS and i + 2 != STEPS:
                quantise(i, 1)
            if block_done is not None:
                add_bias(block_done)
                finish(block_done)
            if 2 <= i <= Z_PASSES + 1:
                add_mean(i - 2)
            if 3 <= i <= Z_PASSES + 1:
                quantise_z(i - 3)
            if 1 <= i <= Z_PASSES:
                scale_noise(i - 1)
            if 2 <= i <= Z_PASSES + 1:
                regroup_z(i - 2)
            if i == Z_PASSES + 1:
                quantise_z(i - 2)
            if i + 1 < STEPS:
                quantise(i + 1, 0)
            if i < Z_PASSES:
                encode(i)
            elif i < STEPS:
                decode(i)
